import numpy as np
import ml_dtypes

BF16 = ml_dtypes.bfloat16


def bf(x):
    return np.asarray(x, np.float32).astype(BF16)


def f32(x):
    return np.asarray(x, np.float32)


def f64(x):
    return np.asarray(x).astype(np.float64)


def striped(idx):
    return np.tile(idx.reshape(-1, 16).T, (8, 1))


CS, D, S, HR, K, N = 256, 128, 512, 256, 4, 1024
EPS = 1e-5


def layer_norm(v, axis):
    mu = v.mean(axis=axis, keepdims=True)
    var = ((v - mu) ** 2).mean(axis=axis, keepdims=True)
    return (v - mu) / np.sqrt(var + EPS)


def sigmoid(v):
    return 1.0 / (1.0 + np.exp(-v))


def setup_inputs():
    idx = np.concatenate([np.random.permutation(S)[:HR] for _ in range(K)])
    return {
        "s": bf(np.random.standard_normal((S, D))),
        "cond_gain": f32(1.0 + 0.1 * np.random.standard_normal((D, 1))),
        "wc1": bf(np.random.standard_normal((D, CS)) / np.sqrt(D)),
        "bc1": f32(0.2 * np.random.standard_normal((CS, 1))),
        "wcn": bf(0.5 * np.random.standard_normal((D, CS)) / np.sqrt(D)),
        "rig": f32(np.random.standard_normal((CS, N))),
        "offs": striped(idx),
    }


def reference(s, cond_gain, wc1, bc1, wcn, rig, offs):
    idx = offs[:16].T.reshape(-1)
    cn = layer_norm(f64(s), 1).T * f64(cond_gain)
    picked = cn[:, idx]
    gate = sigmoid(f64(wc1).T @ picked + f64(bc1))
    shift = f64(wcn).T @ picked
    return layer_norm(f64(rig), 0) * gate + shift

@@ -1,0 +1,137 @@
+import concourse.mybir as mybir
+from concourse.masks import make_identity
+
+F32 = mybir.dt.float32
+BF16 = mybir.dt.bfloat16
+U16 = mybir.dt.uint16
+ALU = mybir.AluOpType
+FUNC = mybir.ActivationFunctionType
+
+P = 128
+S = 512
+D = 128
+CS = 256
+N = 1024
+EPS = 1e-5
+
+S_BLOCKS = S // P
+CH_BLOCKS = CS // P
+CHUNK = 256
+N_CHUNKS = N // CHUNK
+FR_BLOCKS = CHUNK // P
+PIECE_COLS = CHUNK // 16
+STATS = 6
+AGGR = 2
+
+FLOPS = 2 * 2 * D * CS * N
+
+
+def tile_sequenceframetransformerupdate_kernel(tc, s, cond_gain, wc1, bc1, wcn, rig, offs, out):
+    nc = tc.nc
+    rig_view = rig.rearrange("(m p) j -> p m j", p=P)
+    out_view = out.rearrange("(m p) j -> p m j", p=P)
+
+    with (
+        tc.tile_pool(name="held", bufs=1) as held,
+        tc.tile_pool(name="per_chunk", bufs=N_CHUNKS) as per_chunk,
+        tc.tile_pool(name="work", bufs=2) as work,
+        tc.psum_pool(name="psum", bufs=2) as psum,
+    ):
+        s_rows = held.tile([P, S_BLOCKS, D], BF16, name="s_rows")
+        nc.sync.dma_start(s_rows[:], s.rearrange("(b p) d -> p b d", p=P))
+        offsets = held.tile([P, N // 16], U16, name="offsets")
+        nc.sync.dma_start(offsets[:], offs)
+        rig_sb = [held.tile([P, CH_BLOCKS, CHUNK], F32, name=f"rig_sb{c}") for c in range(N_CHUNKS)]
+        for c in range(N_CHUNKS):
+            queue = nc.sync if c % 2 == 0 else nc.scalar
+            queue.dma_start(rig_sb[c][:], rig_view[:, :, c * CHUNK : (c + 1) * CHUNK])
+        wc1_sb = held.tile([D, CS], BF16, name="wc1_sb")
+        nc.scalar.dma_start(wc1_sb[:], wc1)
+        wcn_sb = held.tile([D, CS], BF16, name="wcn_sb")
+        nc.scalar.dma_start(wcn_sb[:], wcn)
+
+        ident = held.tile([P, P], F32, name="ident")
+        make_identity(nc, ident[:])
+        neg_half = held.tile([P, S_BLOCKS, 1], F32, name="neg_half")
+        nc.vector.memset(neg_half[:], -0.5)
+        gain = held.tile([D, 1], F32, name="gain")
+        nc.gpsimd.dma_start(gain[:], cond_gain)
+        bias = [held.tile([P, 1], F32, name=f"bias{m}") for m in range(CH_BLOCKS)]
+        for m in range(CH_BLOCKS):
+            nc.gpsimd.dma_start(bias[m][:], bc1[m * P : (m + 1) * P, :])
+
+        s_stats = held.tile([P, S_BLOCKS, STATS], F32, name="s_stats")
+        s_mv = held.tile([P, S_BLOCKS, AGGR], F32, name="s_mv")
+        for b in range(S_BLOCKS):
+            nc.vector.bn_stats(s_stats[:, b, :], s_rows[:, b, :])
+            nc.vector.bn_aggr(s_mv[:, b, :], s_stats[:, b, :])
+        s_veps = held.tile([P, S_BLOCKS, 1], F32, name="s_veps")
+        nc.vector.tensor_scalar(s_veps[:], s_mv[:, :, 1:2], EPS, None, op0=ALU.add)
+        s_rstd = held.tile([P, S_BLOCKS, 1], F32, name="s_rstd")
+        nc.gpsimd.tensor_tensor(s_rstd[:], s_veps[:], neg_half[:], op=ALU.pow)
+        s_norm = held.tile([P, S_BLOCKS, D], F32, name="s_norm")
+        for b in range(S_BLOCKS):
+            nc.vector.tensor_scalar(
+                s_norm[:, b, :], s_rows[:, b, :], s_mv[:, b, 0:1], s_rstd[:, b, :], op0=ALU.subtract, op1=ALU.mult
+            )
+        sT_ps = psum.tile([D, S], F32, name="sT_ps", tag="flipped")
+        for b in range(S_BLOCKS):
+            nc.tensor.transpose(sT_ps[:, b * P : (b + 1) * P], s_norm[:, b, :], ident[:])
+        cn = held.tile([D, S], BF16, name="cn")
+        nc.scalar.activation(cn[:], sT_ps[:], FUNC.Identity, scale=gain[:, 0:1])
+
+        snT = []
+        for c in range(N_CHUNKS):
+            xT_ps = psum.tile([P, FR_BLOCKS, CS], F32, name="xT_ps", tag="flipped")
+            for q in range(FR_BLOCKS):
+                for m in range(CH_BLOCKS):
+                    nc.tensor.transpose(
+                        xT_ps[:, q, m * P : (m + 1) * P], rig_sb[c][:, m, q * P : (q + 1) * P], ident[:]
+                    )
+            stats = per_chunk.tile([P, FR_BLOCKS, STATS], F32, name="stats")
+            mv = per_chunk.tile([P, FR_BLOCKS, AGGR], F32, name="mv")
+            for q in range(FR_BLOCKS):
+                nc.vector.bn_stats(stats[:, q, :], xT_ps[:, q, :])
+                nc.vector.bn_aggr(mv[:, q, :], stats[:, q, :])
+            veps = per_chunk.tile([P, FR_BLOCKS, 1], F32, name="veps")
+            nc.vector.tensor_scalar(veps[:], mv[:, :, 1:2], EPS, None, op0=ALU.add)
+            neg_mean = per_chunk.tile([P, FR_BLOCKS, 1], F32, name="neg_mean")
+            nc.vector.tensor_scalar(neg_mean[:], mv[:, :, 0:1], -1.0, None, op0=ALU.mult)
+            rstd = per_chunk.tile([P, FR_BLOCKS, 1], F32, name="rstd")
+            nc.gpsimd.tensor_tensor(rstd[:], veps[:], neg_half[:, 0:FR_BLOCKS, :], op=ALU.pow)
+            offset = per_chunk.tile([P, FR_BLOCKS, 1], F32, name="offset")
+            nc.gpsimd.tensor_tensor(offset[:], neg_mean[:], rstd[:], op=ALU.mult)
+            snT_c = per_chunk.tile([P, FR_BLOCKS, CS], F32, name="snT_c")
+            for q in range(FR_BLOCKS):
+                nc.scalar.activation(
+                    snT_c[:, q, :], xT_ps[:, q, :], FUNC.Identity, bias=offset[:, q, :], scale=rstd[:, q, :]
+                )
+            snT.append(snT_c)
+
+        for c in range(N_CHUNKS):
+            piece = offsets[:, c * PIECE_COLS : (c + 1) * PIECE_COLS]
+            gate_ps = psum.tile([P, CH_BLOCKS, CHUNK], F32, name="gate_ps")
+            shift_ps = psum.tile([P, CH_BLOCKS, CHUNK], F32, name="shift_ps")
+            for m in range(CH_BLOCKS):
+                nc.tensor.matmul(
+                    gate_ps[:, m, :], wc1_sb[:, m * P : (m + 1) * P], cn[:].indirect(piece), start=True, stop=True
+                )
+            for m in range(CH_BLOCKS):
+                nc.tensor.matmul(
+                    shift_ps[:, m, :], wcn_sb[:, m * P : (m + 1) * P], cn[:].indirect(piece), start=True, stop=True
+                )
+            gate = work.tile([P, CH_BLOCKS, CHUNK], F32, name="gate")
+            for m in range(CH_BLOCKS):
+                nc.scalar.activation(gate[:, m, :], gate_ps[:, m, :], FUNC.Sigmoid, bias=bias[m][:, 0:1])
+
+            sn_ps = psum.tile([P, CH_BLOCKS, CHUNK], F32, name="sn_ps")
+            for m in range(CH_BLOCKS):
+                for q in range(FR_BLOCKS):
+                    nc.tensor.transpose(
+                        sn_ps[:, m, q * P : (q + 1) * P], snT[c][:, q, m * P : (m + 1) * P], ident[:]
+                    )
+            gated = work.tile([P, CH_BLOCKS, CHUNK], F32, name="gated")
+            nc.vector.tensor_tensor(gated[:], sn_ps[:], gate[:], op=ALU.mult)
+            result = work.tile([P, CH_BLOCKS, CHUNK], F32, name="result")
+            nc.vector.tensor_tensor(result[:], gated[:], shift_ps[:], op=ALU.add)
+            nc.sync.dma_start(out_view[:, :, c * CHUNK : (c + 1) * CHUNK], result[:])

@@ -15,11 +15,14 @@ N = 1024
 EPS = 1e-5
 
 S_BLOCKS = S // P
+S_HALF = S // 2
 CH_BLOCKS = CS // P
 CHUNK = 256
 N_CHUNKS = N // CHUNK
 FR_BLOCKS = CHUNK // P
-PIECE_COLS = CHUNK // 16
+PIECE = 512
+N_PIECES = N // PIECE
+PIECE_COLS = PIECE // 16
 STATS = 6
 AGGR = 2
 
@@ -29,18 +32,19 @@ FLOPS = 2 * 2 * D * CS * N
 def tile_sequenceframetransformerupdate_kernel(tc, s, cond_gain, wc1, bc1, wcn, rig, offs, out):
     nc = tc.nc
     rig_view = rig.rearrange("(m p) j -> p m j", p=P)
-    out_view = out.rearrange("(m p) j -> p m j", p=P)
 
     with (
         tc.tile_pool(name="held", bufs=1) as held,
         tc.tile_pool(name="per_chunk", bufs=N_CHUNKS) as per_chunk,
-        tc.tile_pool(name="work", bufs=2) as work,
-        tc.psum_pool(name="psum", bufs=2) as psum,
+        tc.tile_pool(name="per_piece", bufs=N_PIECES) as per_piece,
+        tc.psum_pool(name="psum", bufs=8) as psum,
     ):
         s_rows = held.tile([P, S_BLOCKS, D], BF16, name="s_rows")
         nc.sync.dma_start(s_rows[:], s.rearrange("(b p) d -> p b d", p=P))
         offsets = held.tile([P, N // 16], U16, name="offsets")
         nc.sync.dma_start(offsets[:], offs)
+        gain = held.tile([D, 1], F32, name="gain")
+        nc.scalar.dma_start(gain[:], cond_gain)
         rig_sb = [held.tile([P, CH_BLOCKS, CHUNK], F32, name=f"rig_sb{c}") for c in range(N_CHUNKS)]
         for c in range(N_CHUNKS):
             queue = nc.sync if c % 2 == 0 else nc.scalar
@@ -49,89 +53,157 @@ def tile_sequenceframetransformerupdate_kernel(tc, s, cond_gain, wc1, bc1, wcn, 
         nc.scalar.dma_start(wc1_sb[:], wc1)
         wcn_sb = held.tile([D, CS], BF16, name="wcn_sb")
         nc.scalar.dma_start(wcn_sb[:], wcn)
+        bias = [held.tile([P, 1], F32, name=f"bias{m}") for m in range(CH_BLOCKS)]
+        for m in range(CH_BLOCKS):
+            nc.scalar.dma_start(bias[m][:], bc1[m * P : (m + 1) * P, :])
 
         ident = held.tile([P, P], F32, name="ident")
         make_identity(nc, ident[:])
-        neg_half = held.tile([P, S_BLOCKS, 1], F32, name="neg_half")
+        neg_half = held.tile([P, FR_BLOCKS, 1], F32, name="neg_half")
         nc.vector.memset(neg_half[:], -0.5)
-        gain = held.tile([D, 1], F32, name="gain")
-        nc.gpsimd.dma_start(gain[:], cond_gain)
-        bias = [held.tile([P, 1], F32, name=f"bias{m}") for m in range(CH_BLOCKS)]
-        for m in range(CH_BLOCKS):
-            nc.gpsimd.dma_start(bias[m][:], bc1[m * P : (m + 1) * P, :])
 
         s_stats = held.tile([P, S_BLOCKS, STATS], F32, name="s_stats")
         s_mv = held.tile([P, S_BLOCKS, AGGR], F32, name="s_mv")
-        for b in range(S_BLOCKS):
-            nc.vector.bn_stats(s_stats[:, b, :], s_rows[:, b, :])
-            nc.vector.bn_aggr(s_mv[:, b, :], s_stats[:, b, :])
         s_veps = held.tile([P, S_BLOCKS, 1], F32, name="s_veps")
-        nc.vector.tensor_scalar(s_veps[:], s_mv[:, :, 1:2], EPS, None, op0=ALU.add)
         s_rstd = held.tile([P, S_BLOCKS, 1], F32, name="s_rstd")
-        nc.gpsimd.tensor_tensor(s_rstd[:], s_veps[:], neg_half[:], op=ALU.pow)
         s_norm = held.tile([P, S_BLOCKS, D], F32, name="s_norm")
-        for b in range(S_BLOCKS):
-            nc.vector.tensor_scalar(
-                s_norm[:, b, :], s_rows[:, b, :], s_mv[:, b, 0:1], s_rstd[:, b, :], op0=ALU.subtract, op1=ALU.mult
-            )
-        sT_ps = psum.tile([D, S], F32, name="sT_ps", tag="flipped")
-        for b in range(S_BLOCKS):
-            nc.tensor.transpose(sT_ps[:, b * P : (b + 1) * P], s_norm[:, b, :], ident[:])
         cn = held.tile([D, S], BF16, name="cn")
-        nc.scalar.activation(cn[:], sT_ps[:], FUNC.Identity, scale=gain[:, 0:1])
+        gate = held.tile([P, CH_BLOCKS, N], F32, name="gate")
+        flipped, mean_var, neg_mean, rstd, offset, snT, sn_ps = {}, {}, {}, {}, {}, {}, {}
+        gate_ps, shift_ps, gated = {}, {}, {}
 
-        snT = []
-        for c in range(N_CHUNKS):
-            xT_ps = psum.tile([P, FR_BLOCKS, CS], F32, name="xT_ps", tag="flipped")
+        def bank(name):
+            return psum.tile([P, PIECE], F32, name=name, tag="bank")
+
+        def residue_stats(half):
+            blocks = slice(2 * half, 2 * half + 2)
+            for b in range(2 * half, 2 * half + 2):
+                nc.vector.bn_stats(s_stats[:, b, :], s_rows[:, b, :])
+                nc.vector.bn_aggr(s_mv[:, b, :], s_stats[:, b, :])
+            nc.vector.tensor_scalar(s_veps[:, blocks, :], s_mv[:, blocks, 1:2], EPS, None, op0=ALU.add)
+            nc.gpsimd.tensor_tensor(s_rstd[:, blocks, :], s_veps[:, blocks, :], neg_half[:], op=ALU.pow)
+
+        def residue_window(half):
+            sT_ps = bank("sT_ps")
+            for k in range(2):
+                b = 2 * half + k
+                nc.vector.tensor_scalar(
+                    s_norm[:, b, :], s_rows[:, b, :], s_mv[:, b, 0:1], s_rstd[:, b, :], op0=ALU.subtract, op1=ALU.mult
+                )
+                nc.tensor.transpose(sT_ps[:, k * P : (k + 1) * P], s_norm[:, b, :], ident[:])
+            nc.scalar.activation(
+                cn[:, half * S_HALF : (half + 1) * S_HALF], sT_ps[:, 0:S_HALF], FUNC.Identity, scale=gain[:, 0:1]
+            )
+
+        def flip_forward(c):
+            flipped[c] = bank("flipped").rearrange("p (q m) -> p q m", q=FR_BLOCKS)
             for q in range(FR_BLOCKS):
                 for m in range(CH_BLOCKS):
                     nc.tensor.transpose(
-                        xT_ps[:, q, m * P : (m + 1) * P], rig_sb[c][:, m, q * P : (q + 1) * P], ident[:]
+                        flipped[c][:, q, m * P : (m + 1) * P], rig_sb[c][:, m, q * P : (q + 1) * P], ident[:]
                     )
+
+        def frame_stats(c):
             stats = per_chunk.tile([P, FR_BLOCKS, STATS], F32, name="stats")
-            mv = per_chunk.tile([P, FR_BLOCKS, AGGR], F32, name="mv")
+            mean_var[c] = per_chunk.tile([P, FR_BLOCKS, AGGR], F32, name="mean_var")
             for q in range(FR_BLOCKS):
-                nc.vector.bn_stats(stats[:, q, :], xT_ps[:, q, :])
-                nc.vector.bn_aggr(mv[:, q, :], stats[:, q, :])
+                nc.vector.bn_stats(stats[:, q, :], flipped[c][:, q, :])
+                nc.vector.bn_aggr(mean_var[c][:, q, :], stats[:, q, :])
             veps = per_chunk.tile([P, FR_BLOCKS, 1], F32, name="veps")
-            nc.vector.tensor_scalar(veps[:], mv[:, :, 1:2], EPS, None, op0=ALU.add)
-            neg_mean = per_chunk.tile([P, FR_BLOCKS, 1], F32, name="neg_mean")
-            nc.vector.tensor_scalar(neg_mean[:], mv[:, :, 0:1], -1.0, None, op0=ALU.mult)
-            rstd = per_chunk.tile([P, FR_BLOCKS, 1], F32, name="rstd")
-            nc.gpsimd.tensor_tensor(rstd[:], veps[:], neg_half[:, 0:FR_BLOCKS, :], op=ALU.pow)
-            offset = per_chunk.tile([P, FR_BLOCKS, 1], F32, name="offset")
-            nc.gpsimd.tensor_tensor(offset[:], neg_mean[:], rstd[:], op=ALU.mult)
-            snT_c = per_chunk.tile([P, FR_BLOCKS, CS], F32, name="snT_c")
+            nc.vector.tensor_scalar(veps[:], mean_var[c][:, :, 1:2], EPS, None, op0=ALU.add)
+            rstd[c] = per_chunk.tile([P, FR_BLOCKS, 1], F32, name="rstd")
+            nc.gpsimd.tensor_tensor(rstd[c][:], veps[:], neg_half[:], op=ALU.pow)
+            neg_mean[c] = per_chunk.tile([P, FR_BLOCKS, 1], F32, name="neg_mean")
+            nc.vector.tensor_scalar(neg_mean[c][:], mean_var[c][:, :, 0:1], -1.0, None, op0=ALU.mult)
+
+        def frame_offset(c):
+            offset[c] = per_chunk.tile([P, FR_BLOCKS, 1], F32, name="offset")
+            nc.vector.tensor_tensor(offset[c][:], neg_mean[c][:], rstd[c][:], op=ALU.mult)
+
+        def normalise(c):
+            snT[c] = per_chunk.tile([P, FR_BLOCKS, CS], F32, name="snT")
             for q in range(FR_BLOCKS):
                 nc.scalar.activation(
-                    snT_c[:, q, :], xT_ps[:, q, :], FUNC.Identity, bias=offset[:, q, :], scale=rstd[:, q, :]
+                    snT[c][:, q, :], flipped[c][:, q, :], FUNC.Identity, bias=offset[c][:, q, :], scale=rstd[c][:, q, :]
                 )
-            snT.append(snT_c)
 
-        for c in range(N_CHUNKS):
-            piece = offsets[:, c * PIECE_COLS : (c + 1) * PIECE_COLS]
-            gate_ps = psum.tile([P, CH_BLOCKS, CHUNK], F32, name="gate_ps")
-            shift_ps = psum.tile([P, CH_BLOCKS, CHUNK], F32, name="shift_ps")
-            for m in range(CH_BLOCKS):
-                nc.tensor.matmul(
-                    gate_ps[:, m, :], wc1_sb[:, m * P : (m + 1) * P], cn[:].indirect(piece), start=True, stop=True
-                )
-            for m in range(CH_BLOCKS):
-                nc.tensor.matmul(
-                    shift_ps[:, m, :], wcn_sb[:, m * P : (m + 1) * P], cn[:].indirect(piece), start=True, stop=True
-                )
-            gate = work.tile([P, CH_BLOCKS, CHUNK], F32, name="gate")
-            for m in range(CH_BLOCKS):
-                nc.scalar.activation(gate[:, m, :], gate_ps[:, m, :], FUNC.Sigmoid, bias=bias[m][:, 0:1])
-
-            sn_ps = psum.tile([P, CH_BLOCKS, CHUNK], F32, name="sn_ps")
+        def flip_back(c):
+            sn_ps[c] = bank("sn_ps").rearrange("p (m j) -> p m j", m=CH_BLOCKS)
             for m in range(CH_BLOCKS):
                 for q in range(FR_BLOCKS):
                     nc.tensor.transpose(
-                        sn_ps[:, m, q * P : (q + 1) * P], snT[c][:, q, m * P : (m + 1) * P], ident[:]
+                        sn_ps[c][:, m, q * P : (q + 1) * P], snT[c][:, q, m * P : (m + 1) * P], ident[:]
                     )
-            gated = work.tile([P, CH_BLOCKS, CHUNK], F32, name="gated")
-            nc.vector.tensor_tensor(gated[:], sn_ps[:], gate[:], op=ALU.mult)
-            result = work.tile([P, CH_BLOCKS, CHUNK], F32, name="result")
-            nc.vector.tensor_tensor(result[:], gated[:], shift_ps[:], op=ALU.add)
-            nc.sync.dma_start(out_view[:, :, c * CHUNK : (c + 1) * CHUNK], result[:])
+
+        def project(weights, h, m, name):
+            product = bank(name)
+            piece = offsets[:, h * PIECE_COLS : (h + 1) * PIECE_COLS]
+            nc.tensor.matmul(product[:], weights[:, m * P : (m + 1) * P], cn[:].indirect(piece), start=True, stop=True)
+            return product
+
+        def sigmoid(h, m):
+            nc.scalar.activation(
+                gate[:, m, h * PIECE : (h + 1) * PIECE], gate_ps[h, m][:], FUNC.Sigmoid, bias=bias[m][:, 0:1]
+            )
+
+        def apply_gate(c):
+            h, part = divmod(c, N_CHUNKS // N_PIECES)
+            if part == 0:
+                gated[h] = per_piece.tile([P, CH_BLOCKS, PIECE], F32, name="gated")
+            nc.vector.tensor_tensor(
+                gated[h][:, :, part * CHUNK : (part + 1) * CHUNK],
+                sn_ps[c][:],
+                gate[:, :, c * CHUNK : (c + 1) * CHUNK],
+                op=ALU.mult,
+            )
+
+        def add_shift(h, m):
+            result = per_chunk.tile([P, PIECE], F32, name="result")
+            nc.vector.tensor_tensor(result[:], gated[h][:, m, :], shift_ps[h, m][:], op=ALU.add)
+            nc.sync.dma_start(out[m * P : (m + 1) * P, h * PIECE : (h + 1) * PIECE], result[:])
+
+        residue_stats(0)
+        residue_stats(1)
+        flip_forward(0)
+        flip_forward(1)
+        residue_window(0)
+        flip_forward(2)
+        residue_window(1)
+        flip_forward(3)
+
+        frame_stats(0)
+        frame_stats(1)
+        frame_offset(0)
+        gate_ps[0, 0] = project(wc1_sb, 0, 0, "gate_ps")
+        gate_ps[0, 1] = project(wc1_sb, 0, 1, "gate_ps")
+        sigmoid(0, 0)
+        shift_ps[0, 0] = project(wcn_sb, 0, 0, "shift_ps")
+        normalise(0)
+        flip_back(0)
+        sigmoid(0, 1)
+        shift_ps[0, 1] = project(wcn_sb, 0, 1, "shift_ps")
+        frame_stats(2)
+        frame_offset(1)
+        normalise(1)
+        flip_back(1)
+        frame_stats(3)
+        frame_offset(2)
+        apply_gate(0)
+        frame_offset(3)
+        normalise(2)
+        normalise(3)
+        gate_ps[1, 0] = project(wc1_sb, 1, 0, "gate_ps")
+        gate_ps[1, 1] = project(wc1_sb, 1, 1, "gate_ps")
+        sigmoid(1, 0)
+        sigmoid(1, 1)
+        flip_back(2)
+        flip_back(3)
+        shift_ps[1, 0] = project(wcn_sb, 1, 0, "shift_ps")
+        shift_ps[1, 1] = project(wcn_sb, 1, 1, "shift_ps")
+        apply_gate(1)
+        add_shift(0, 0)
+        add_shift(0, 1)
+        apply_gate(2)
+        apply_gate(3)
+        add_shift(1, 0)
+        add_shift(1, 1)

@@ -39,51 +39,60 @@ def tile_sequenceframetransformerupdate_kernel(tc, s, cond_gain, wc1, bc1, wcn, 
         tc.tile_pool(name="per_piece", bufs=N_PIECES) as per_piece,
         tc.psum_pool(name="psum", bufs=8) as psum,
     ):
-        s_rows = held.tile([P, S_BLOCKS, D], BF16, name="s_rows")
-        nc.sync.dma_start(s_rows[:], s.rearrange("(b p) d -> p b d", p=P))
-        offsets = held.tile([P, N // 16], U16, name="offsets")
-        nc.sync.dma_start(offsets[:], offs)
         gain = held.tile([D, 1], F32, name="gain")
         nc.scalar.dma_start(gain[:], cond_gain)
+        bias = held.tile([P, CH_BLOCKS], F32, name="bias")
+        with nc.allow_non_contiguous_dma(reason="256 biases, one to a partition and channel block"):
+            nc.scalar.dma_start(bias[:], bc1.rearrange("(m p) o -> p (m o)", p=P))
+        s_rows = held.tile([P, S_BLOCKS, D], BF16, name="s_rows")
+        nc.sync.dma_start(s_rows[:], s.rearrange("(b p) d -> p b d", p=P))
         rig_sb = [held.tile([P, CH_BLOCKS, CHUNK], F32, name=f"rig_sb{c}") for c in range(N_CHUNKS)]
-        for c in range(N_CHUNKS):
-            queue = nc.sync if c % 2 == 0 else nc.scalar
-            queue.dma_start(rig_sb[c][:], rig_view[:, :, c * CHUNK : (c + 1) * CHUNK])
+        offsets = held.tile([P, N // 16], U16, name="offsets")
         wc1_sb = held.tile([D, CS], BF16, name="wc1_sb")
-        nc.scalar.dma_start(wc1_sb[:], wc1)
         wcn_sb = held.tile([D, CS], BF16, name="wcn_sb")
-        nc.scalar.dma_start(wcn_sb[:], wcn)
-        bias = [held.tile([P, 1], F32, name=f"bias{m}") for m in range(CH_BLOCKS)]
-        for m in range(CH_BLOCKS):
-            nc.scalar.dma_start(bias[m][:], bc1[m * P : (m + 1) * P, :])
+        for c in range(N_CHUNKS):
+            if c == N_CHUNKS // 2:
+                nc.sync.dma_start(offsets[:], offs)
+                nc.sync.dma_start(wc1_sb[:], wc1)
+                nc.sync.dma_start(wcn_sb[:], wcn)
+            nc.sync.dma_start(rig_sb[c][:], rig_view[:, :, c * CHUNK : (c + 1) * CHUNK])
 
         ident = held.tile([P, P], F32, name="ident")
         make_identity(nc, ident[:])
         neg_half = held.tile([P, FR_BLOCKS, 1], F32, name="neg_half")
         nc.vector.memset(neg_half[:], -0.5)
+        eps_col = held.tile([P, 1], F32, name="eps_col")
+        nc.vector.memset(eps_col[:], EPS)
 
         s_stats = held.tile([P, S_BLOCKS, STATS], F32, name="s_stats")
         s_mv = held.tile([P, S_BLOCKS, AGGR], F32, name="s_mv")
-        s_veps = held.tile([P, S_BLOCKS, 1], F32, name="s_veps")
+        s_std = held.tile([P, S_BLOCKS, 1], F32, name="s_std")
         s_rstd = held.tile([P, S_BLOCKS, 1], F32, name="s_rstd")
         s_norm = held.tile([P, S_BLOCKS, D], F32, name="s_norm")
         cn = held.tile([D, S], BF16, name="cn")
         gate = held.tile([P, CH_BLOCKS, N], F32, name="gate")
-        flipped, mean_var, neg_mean, rstd, offset, snT, sn_ps = {}, {}, {}, {}, {}, {}, {}
+        flipped, stats, mean_var, neg_mean, rstd, offset, snT, sn_ps = {}, {}, {}, {}, {}, {}, {}, {}
         gate_ps, shift_ps, gated = {}, {}, {}
 
         def bank(name):
             return psum.tile([P, PIECE], F32, name=name, tag="bank")
 
-        def residue_stats(half):
-            blocks = slice(2 * half, 2 * half + 2)
-            for b in range(2 * half, 2 * half + 2):
+        def load_table_of(func, column, name):
+            scratch = held.tile([P, 1], F32, name=name)
+            nc.scalar.activation(scratch[:], column, func)
+
+        def residue_moments(half):
+            blocks = range(2 * half, 2 * half + 2)
+            for b in blocks:
                 nc.vector.bn_stats(s_stats[:, b, :], s_rows[:, b, :])
+            for b in blocks:
                 nc.vector.bn_aggr(s_mv[:, b, :], s_stats[:, b, :])
-            nc.vector.tensor_scalar(s_veps[:, blocks, :], s_mv[:, blocks, 1:2], EPS, None, op0=ALU.add)
-            nc.gpsimd.tensor_tensor(s_rstd[:, blocks, :], s_veps[:, blocks, :], neg_half[:], op=ALU.pow)
+            both = slice(2 * half, 2 * half + 2)
+            nc.scalar.activation(s_std[:, both, :], s_mv[:, both, 1:2], FUNC.Sqrt, bias=eps_col[:, 0:1])
 
         def residue_window(half):
+            both = slice(2 * half, 2 * half + 2)
+            nc.vector.reciprocal(s_rstd[:, both, :], s_std[:, both, :])
             sT_ps = bank("sT_ps")
             for k in range(2):
                 b = 2 * half + k
@@ -103,12 +112,13 @@ def tile_sequenceframetransformerupdate_kernel(tc, s, cond_gain, wc1, bc1, wcn, 
                         flipped[c][:, q, m * P : (m + 1) * P], rig_sb[c][:, m, q * P : (q + 1) * P], ident[:]
                     )
 
-        def frame_stats(c):
-            stats = per_chunk.tile([P, FR_BLOCKS, STATS], F32, name="stats")
+        def frame_moments(c):
+            stats[c] = per_chunk.tile([P, FR_BLOCKS, STATS], F32, name="stats")
             mean_var[c] = per_chunk.tile([P, FR_BLOCKS, AGGR], F32, name="mean_var")
             for q in range(FR_BLOCKS):
-                nc.vector.bn_stats(stats[:, q, :], flipped[c][:, q, :])
-                nc.vector.bn_aggr(mean_var[c][:, q, :], stats[:, q, :])
+                nc.vector.bn_stats(stats[c][:, q, :], flipped[c][:, q, :])
+            for q in range(FR_BLOCKS):
+                nc.vector.bn_aggr(mean_var[c][:, q, :], stats[c][:, q, :])
             veps = per_chunk.tile([P, FR_BLOCKS, 1], F32, name="veps")
             nc.vector.tensor_scalar(veps[:], mean_var[c][:, :, 1:2], EPS, None, op0=ALU.add)
             rstd[c] = per_chunk.tile([P, FR_BLOCKS, 1], F32, name="rstd")
@@ -118,7 +128,7 @@ def tile_sequenceframetransformerupdate_kernel(tc, s, cond_gain, wc1, bc1, wcn, 
 
         def frame_offset(c):
             offset[c] = per_chunk.tile([P, FR_BLOCKS, 1], F32, name="offset")
-            nc.vector.tensor_tensor(offset[c][:], neg_mean[c][:], rstd[c][:], op=ALU.mult)
+            nc.gpsimd.tensor_tensor(offset[c][:], neg_mean[c][:], rstd[c][:], op=ALU.mult)
 
         def normalise(c):
             snT[c] = per_chunk.tile([P, FR_BLOCKS, CS], F32, name="snT")
@@ -143,7 +153,7 @@ def tile_sequenceframetransformerupdate_kernel(tc, s, cond_gain, wc1, bc1, wcn, 
 
         def sigmoid(h, m):
             nc.scalar.activation(
-                gate[:, m, h * PIECE : (h + 1) * PIECE], gate_ps[h, m][:], FUNC.Sigmoid, bias=bias[m][:, 0:1]
+                gate[:, m, h * PIECE : (h + 1) * PIECE], gate_ps[h, m][:], FUNC.Sigmoid, bias=bias[:, m : m + 1]
             )
 
         def apply_gate(c):
@@ -158,46 +168,51 @@ def tile_sequenceframetransformerupdate_kernel(tc, s, cond_gain, wc1, bc1, wcn, 
             )
 
         def add_shift(h, m):
-            result = per_chunk.tile([P, PIECE], F32, name="result")
-            nc.vector.tensor_tensor(result[:], gated[h][:, m, :], shift_ps[h, m][:], op=ALU.add)
-            nc.sync.dma_start(out[m * P : (m + 1) * P, h * PIECE : (h + 1) * PIECE], result[:])
+            for part in range(PIECE // CHUNK):
+                cols = slice(part * CHUNK, (part + 1) * CHUNK)
+                result = per_chunk.tile([P, CHUNK], F32, name="result")
+                nc.vector.tensor_tensor(result[:], gated[h][:, m, cols], shift_ps[h, m][:, cols], op=ALU.add)
+                first = h * PIECE + part * CHUNK
+                nc.sync.dma_start(out[m * P : (m + 1) * P, first : first + CHUNK], result[:])
 
-        residue_stats(0)
-        residue_stats(1)
+        load_table_of(FUNC.Sqrt, eps_col[:], "scratch_sqrt")
         flip_forward(0)
         flip_forward(1)
+        residue_moments(0)
+        residue_moments(1)
+        load_table_of(FUNC.Sigmoid, s_std[:, S_BLOCKS - 1, :], "scratch_sigmoid")
         residue_window(0)
-        flip_forward(2)
         residue_window(1)
+        flip_forward(2)
         flip_forward(3)
 
-        frame_stats(0)
-        frame_stats(1)
+        frame_moments(0)
         frame_offset(0)
+        frame_moments(1)
+        frame_offset(1)
         gate_ps[0, 0] = project(wc1_sb, 0, 0, "gate_ps")
         gate_ps[0, 1] = project(wc1_sb, 0, 1, "gate_ps")
+        normalise(0)
         sigmoid(0, 0)
         shift_ps[0, 0] = project(wcn_sb, 0, 0, "shift_ps")
-        normalise(0)
         flip_back(0)
         sigmoid(0, 1)
         shift_ps[0, 1] = project(wcn_sb, 0, 1, "shift_ps")
-        frame_stats(2)
-        frame_offset(1)
+        frame_moments(2)
+        frame_offset(2)
         normalise(1)
         flip_back(1)
-        frame_stats(3)
-        frame_offset(2)
-        apply_gate(0)
+        frame_moments(3)
         frame_offset(3)
+        apply_gate(0)
         normalise(2)
         normalise(3)
         gate_ps[1, 0] = project(wc1_sb, 1, 0, "gate_ps")
         gate_ps[1, 1] = project(wc1_sb, 1, 1, "gate_ps")
-        sigmoid(1, 0)
-        sigmoid(1, 1)
         flip_back(2)
         flip_back(3)
+        sigmoid(1, 0)
+        sigmoid(1, 1)
         shift_ps[1, 0] = project(wcn_sb, 1, 0, "shift_ps")
         shift_ps[1, 1] = project(wcn_sb, 1, 1, "shift_ps")
         apply_gate(1)

@@ -15,7 +15,9 @@ N = 1024
 EPS = 1e-5
 
 S_BLOCKS = S // P
-S_HALF = S // 2
+S_PARTS = 2
+PART = S // S_PARTS
+PART_BLOCKS = S_BLOCKS // S_PARTS
 CH_BLOCKS = CS // P
 CHUNK = 256
 N_CHUNKS = N // CHUNK
@@ -23,7 +25,10 @@ FR_BLOCKS = CHUNK // P
 PIECE = 512
 N_PIECES = N // PIECE
 PIECE_COLS = PIECE // 16
-STATS = 6
+PIECE_CHUNKS = PIECE // CHUNK
+BANKS = 8
+GROUP = 3
+STATS = 2 * GROUP
 AGGR = 2
 
 FLOPS = 2 * 2 * D * CS * N
@@ -37,7 +42,7 @@ def tile_sequenceframetransformerupdate_kernel(tc, s, cond_gain, wc1, bc1, wcn, 
         tc.tile_pool(name="held", bufs=1) as held,
         tc.tile_pool(name="per_chunk", bufs=N_CHUNKS) as per_chunk,
         tc.tile_pool(name="per_piece", bufs=N_PIECES) as per_piece,
-        tc.psum_pool(name="psum", bufs=8) as psum,
+        tc.psum_pool(name="psum", bufs=BANKS) as psum,
     ):
         gain = held.tile([D, 1], F32, name="gain")
         nc.scalar.dma_start(gain[:], cond_gain)
@@ -47,15 +52,14 @@ def tile_sequenceframetransformerupdate_kernel(tc, s, cond_gain, wc1, bc1, wcn, 
         s_rows = held.tile([P, S_BLOCKS, D], BF16, name="s_rows")
         nc.sync.dma_start(s_rows[:], s.rearrange("(b p) d -> p b d", p=P))
         rig_sb = [held.tile([P, CH_BLOCKS, CHUNK], F32, name=f"rig_sb{c}") for c in range(N_CHUNKS)]
-        offsets = held.tile([P, N // 16], U16, name="offsets")
-        wc1_sb = held.tile([D, CS], BF16, name="wc1_sb")
-        wcn_sb = held.tile([D, CS], BF16, name="wcn_sb")
         for c in range(N_CHUNKS):
-            if c == N_CHUNKS // 2:
-                nc.sync.dma_start(offsets[:], offs)
-                nc.sync.dma_start(wc1_sb[:], wc1)
-                nc.sync.dma_start(wcn_sb[:], wcn)
             nc.sync.dma_start(rig_sb[c][:], rig_view[:, :, c * CHUNK : (c + 1) * CHUNK])
+        offsets = held.tile([P, N // 16], U16, name="offsets")
+        nc.sync.dma_start(offsets[:], offs)
+        wc1_sb = held.tile([D, CS], BF16, name="wc1_sb")
+        nc.sync.dma_start(wc1_sb[:], wc1)
+        wcn_sb = held.tile([D, CS], BF16, name="wcn_sb")
+        nc.sync.dma_start(wcn_sb[:], wcn)
 
         ident = held.tile([P, P], F32, name="ident")
         make_identity(nc, ident[:])
@@ -63,16 +67,20 @@ def tile_sequenceframetransformerupdate_kernel(tc, s, cond_gain, wc1, bc1, wcn, 
         nc.vector.memset(neg_half[:], -0.5)
         eps_col = held.tile([P, 1], F32, name="eps_col")
         nc.vector.memset(eps_col[:], EPS)
+        frame_stats = held.tile([P, N // P, STATS + GROUP], F32, name="frame_stats")
+        nc.vector.memset(frame_stats[:, :, STATS : STATS + 2], 0.0)
+        nc.vector.memset(frame_stats[:, :, STATS + 2 : STATS + GROUP], CS * EPS)
 
         s_stats = held.tile([P, S_BLOCKS, STATS], F32, name="s_stats")
-        s_mv = held.tile([P, S_BLOCKS, AGGR], F32, name="s_mv")
+        s_mean_var = held.tile([P, S_BLOCKS, AGGR], F32, name="s_mean_var")
         s_std = held.tile([P, S_BLOCKS, 1], F32, name="s_std")
         s_rstd = held.tile([P, S_BLOCKS, 1], F32, name="s_rstd")
         s_norm = held.tile([P, S_BLOCKS, D], F32, name="s_norm")
         cn = held.tile([D, S], BF16, name="cn")
         gate = held.tile([P, CH_BLOCKS, N], F32, name="gate")
-        flipped, stats, mean_var, neg_mean, rstd, offset, snT, sn_ps = {}, {}, {}, {}, {}, {}, {}, {}
-        gate_ps, shift_ps, gated = {}, {}, {}
+        flipped, rstd, offset, snT, sn_ps = {}, {}, {}, {}, {}
+        gate_ps, shift_ps = {}, {}
+        gated = {}
 
         def bank(name):
             return psum.tile([P, PIECE], F32, name=name, tag="bank")
@@ -81,27 +89,32 @@ def tile_sequenceframetransformerupdate_kernel(tc, s, cond_gain, wc1, bc1, wcn, 
             scratch = held.tile([P, 1], F32, name=name)
             nc.scalar.activation(scratch[:], column, func)
 
-        def residue_moments(half):
-            blocks = range(2 * half, 2 * half + 2)
+        def residue_moments(part):
+            blocks = range(part * PART_BLOCKS, (part + 1) * PART_BLOCKS)
             for b in blocks:
                 nc.vector.bn_stats(s_stats[:, b, :], s_rows[:, b, :])
             for b in blocks:
-                nc.vector.bn_aggr(s_mv[:, b, :], s_stats[:, b, :])
-            both = slice(2 * half, 2 * half + 2)
-            nc.scalar.activation(s_std[:, both, :], s_mv[:, both, 1:2], FUNC.Sqrt, bias=eps_col[:, 0:1])
+                nc.vector.bn_aggr(s_mean_var[:, b, :], s_stats[:, b, :])
+            both = slice(part * PART_BLOCKS, (part + 1) * PART_BLOCKS)
+            nc.scalar.activation(s_std[:, both, :], s_mean_var[:, both, 1:2], FUNC.Sqrt, bias=eps_col[:, 0:1])
 
-        def residue_window(half):
-            both = slice(2 * half, 2 * half + 2)
+        def residue_window(part):
+            both = slice(part * PART_BLOCKS, (part + 1) * PART_BLOCKS)
             nc.vector.reciprocal(s_rstd[:, both, :], s_std[:, both, :])
             sT_ps = bank("sT_ps")
-            for k in range(2):
-                b = 2 * half + k
+            for k in range(PART_BLOCKS):
+                b = part * PART_BLOCKS + k
                 nc.vector.tensor_scalar(
-                    s_norm[:, b, :], s_rows[:, b, :], s_mv[:, b, 0:1], s_rstd[:, b, :], op0=ALU.subtract, op1=ALU.mult
+                    s_norm[:, b, :],
+                    s_rows[:, b, :],
+                    s_mean_var[:, b, 0:1],
+                    s_rstd[:, b, :],
+                    op0=ALU.subtract,
+                    op1=ALU.mult,
                 )
                 nc.tensor.transpose(sT_ps[:, k * P : (k + 1) * P], s_norm[:, b, :], ident[:])
             nc.scalar.activation(
-                cn[:, half * S_HALF : (half + 1) * S_HALF], sT_ps[:, 0:S_HALF], FUNC.Identity, scale=gain[:, 0:1]
+                cn[:, part * PART : (part + 1) * PART], sT_ps[:, 0:PART], FUNC.Identity, scale=gain[:, 0:1]
             )
 
         def flip_forward(c):
@@ -113,22 +126,17 @@ def tile_sequenceframetransformerupdate_kernel(tc, s, cond_gain, wc1, bc1, wcn, 
                     )
 
         def frame_moments(c):
-            stats[c] = per_chunk.tile([P, FR_BLOCKS, STATS], F32, name="stats")
-            mean_var[c] = per_chunk.tile([P, FR_BLOCKS, AGGR], F32, name="mean_var")
+            mean_var = per_chunk.tile([P, FR_BLOCKS, AGGR], F32, name="mean_var")
             for q in range(FR_BLOCKS):
-                nc.vector.bn_stats(stats[c][:, q, :], flipped[c][:, q, :])
+                nc.vector.bn_stats(frame_stats[:, c * FR_BLOCKS + q, 0:STATS], flipped[c][:, q, :])
             for q in range(FR_BLOCKS):
-                nc.vector.bn_aggr(mean_var[c][:, q, :], stats[c][:, q, :])
-            veps = per_chunk.tile([P, FR_BLOCKS, 1], F32, name="veps")
-            nc.vector.tensor_scalar(veps[:], mean_var[c][:, :, 1:2], EPS, None, op0=ALU.add)
+                nc.vector.bn_aggr(mean_var[:, q, :], frame_stats[:, c * FR_BLOCKS + q, :])
             rstd[c] = per_chunk.tile([P, FR_BLOCKS, 1], F32, name="rstd")
-            nc.gpsimd.tensor_tensor(rstd[c][:], veps[:], neg_half[:], op=ALU.pow)
-            neg_mean[c] = per_chunk.tile([P, FR_BLOCKS, 1], F32, name="neg_mean")
-            nc.vector.tensor_scalar(neg_mean[c][:], mean_var[c][:, :, 0:1], -1.0, None, op0=ALU.mult)
-
-        def frame_offset(c):
+            nc.gpsimd.tensor_tensor(rstd[c][:], mean_var[:, :, 1:2], neg_half[:], op=ALU.pow)
+            neg_mean = per_chunk.tile([P, FR_BLOCKS, 1], F32, name="neg_mean")
+            nc.vector.tensor_scalar(neg_mean[:], mean_var[:, :, 0:1], -1.0, None, op0=ALU.mult)
             offset[c] = per_chunk.tile([P, FR_BLOCKS, 1], F32, name="offset")
-            nc.gpsimd.tensor_tensor(offset[c][:], neg_mean[c][:], rstd[c][:], op=ALU.mult)
+            nc.gpsimd.tensor_tensor(offset[c][:], neg_mean[:], rstd[c][:], op=ALU.mult)
 
         def normalise(c):
             snT[c] = per_chunk.tile([P, FR_BLOCKS, CS], F32, name="snT")
@@ -156,10 +164,8 @@ def tile_sequenceframetransformerupdate_kernel(tc, s, cond_gain, wc1, bc1, wcn, 
                 gate[:, m, h * PIECE : (h + 1) * PIECE], gate_ps[h, m][:], FUNC.Sigmoid, bias=bias[:, m : m + 1]
             )
 
-        def apply_gate(c):
-            h, part = divmod(c, N_CHUNKS // N_PIECES)
-            if part == 0:
-                gated[h] = per_piece.tile([P, CH_BLOCKS, PIECE], F32, name="gated")
+        def apply_gate(h, part):
+            c = h * PIECE_CHUNKS + part
             nc.vector.tensor_tensor(
                 gated[h][:, :, part * CHUNK : (part + 1) * CHUNK],
                 sn_ps[c][:],
@@ -168,7 +174,7 @@ def tile_sequenceframetransformerupdate_kernel(tc, s, cond_gain, wc1, bc1, wcn, 
             )
 
         def add_shift(h, m):
-            for part in range(PIECE // CHUNK):
+            for part in range(PIECE_CHUNKS):
                 cols = slice(part * CHUNK, (part + 1) * CHUNK)
                 result = per_chunk.tile([P, CHUNK], F32, name="result")
                 nc.vector.tensor_tensor(result[:], gated[h][:, m, cols], shift_ps[h, m][:, cols], op=ALU.add)
@@ -176,49 +182,27 @@ def tile_sequenceframetransformerupdate_kernel(tc, s, cond_gain, wc1, bc1, wcn, 
                 nc.sync.dma_start(out[m * P : (m + 1) * P, first : first + CHUNK], result[:])
 
         load_table_of(FUNC.Sqrt, eps_col[:], "scratch_sqrt")
-        flip_forward(0)
-        flip_forward(1)
-        residue_moments(0)
-        residue_moments(1)
+        for part in range(S_PARTS):
+            residue_moments(part)
         load_table_of(FUNC.Sigmoid, s_std[:, S_BLOCKS - 1, :], "scratch_sigmoid")
-        residue_window(0)
-        residue_window(1)
-        flip_forward(2)
-        flip_forward(3)
-
-        frame_moments(0)
-        frame_offset(0)
-        frame_moments(1)
-        frame_offset(1)
-        gate_ps[0, 0] = project(wc1_sb, 0, 0, "gate_ps")
-        gate_ps[0, 1] = project(wc1_sb, 0, 1, "gate_ps")
-        normalise(0)
-        sigmoid(0, 0)
-        shift_ps[0, 0] = project(wcn_sb, 0, 0, "shift_ps")
-        flip_back(0)
-        sigmoid(0, 1)
-        shift_ps[0, 1] = project(wcn_sb, 0, 1, "shift_ps")
-        frame_moments(2)
-        frame_offset(2)
-        normalise(1)
-        flip_back(1)
-        frame_moments(3)
-        frame_offset(3)
-        apply_gate(0)
-        normalise(2)
-        normalise(3)
-        gate_ps[1, 0] = project(wc1_sb, 1, 0, "gate_ps")
-        gate_ps[1, 1] = project(wc1_sb, 1, 1, "gate_ps")
-        flip_back(2)
-        flip_back(3)
-        sigmoid(1, 0)
-        sigmoid(1, 1)
-        shift_ps[1, 0] = project(wcn_sb, 1, 0, "shift_ps")
-        shift_ps[1, 1] = project(wcn_sb, 1, 1, "shift_ps")
-        apply_gate(1)
-        add_shift(0, 0)
-        add_shift(0, 1)
-        apply_gate(2)
-        apply_gate(3)
-        add_shift(1, 0)
-        add_shift(1, 1)
+        for part in range(S_PARTS):
+            residue_window(part)
+        for c in range(N_CHUNKS):
+            flip_forward(c)
+        for c in range(N_CHUNKS):
+            frame_moments(c)
+        for h in range(N_PIECES):
+            for m in range(CH_BLOCKS):
+                gate_ps[h, m] = project(wc1_sb, h, m, "gate_ps")
+            for part in range(PIECE_CHUNKS):
+                normalise(h * PIECE_CHUNKS + part)
+                flip_back(h * PIECE_CHUNKS + part)
+            for m in range(CH_BLOCKS):
+                sigmoid(h, m)
+            for m in range(CH_BLOCKS):
+                shift_ps[h, m] = project(wcn_sb, h, m, "shift_ps")
+            gated[h] = per_piece.tile([P, CH_BLOCKS, PIECE], F32, name="gated")
+            for part in range(PIECE_CHUNKS):
+                apply_gate(h, part)
+            for m in range(CH_BLOCKS):
+                add_shift(h, m)

@@ -21,6 +21,7 @@ PART_BLOCKS = S_BLOCKS // S_PARTS
 CH_BLOCKS = CS // P
 CHUNK = 256
 N_CHUNKS = N // CHUNK
+EARLY_CHUNKS = 2
 FR_BLOCKS = CHUNK // P
 PIECE = 512
 N_PIECES = N // PIECE
@@ -182,25 +183,30 @@ def tile_sequenceframetransformerupdate_kernel(tc, s, cond_gain, wc1, bc1, wcn, 
                 nc.sync.dma_start(out[m * P : (m + 1) * P, first : first + CHUNK], result[:])
 
         load_table_of(FUNC.Sqrt, eps_col[:], "scratch_sqrt")
+        for c in range(EARLY_CHUNKS):
+            flip_forward(c)
         for part in range(S_PARTS):
             residue_moments(part)
         load_table_of(FUNC.Sigmoid, s_std[:, S_BLOCKS - 1, :], "scratch_sigmoid")
         for part in range(S_PARTS):
             residue_window(part)
-        for c in range(N_CHUNKS):
+        for c in range(EARLY_CHUNKS, N_CHUNKS):
             flip_forward(c)
         for c in range(N_CHUNKS):
             frame_moments(c)
         for h in range(N_PIECES):
+            chunks = range(h * PIECE_CHUNKS, (h + 1) * PIECE_CHUNKS)
+            for c in chunks:
+                normalise(c)
             for m in range(CH_BLOCKS):
                 gate_ps[h, m] = project(wc1_sb, h, m, "gate_ps")
-            for part in range(PIECE_CHUNKS):
-                normalise(h * PIECE_CHUNKS + part)
-                flip_back(h * PIECE_CHUNKS + part)
+            for c in chunks:
+                flip_back(c)
             for m in range(CH_BLOCKS):
                 sigmoid(h, m)
             for m in range(CH_BLOCKS):
                 shift_ps[h, m] = project(wcn_sb, h, m, "shift_ps")
+        for h in range(N_PIECES):
             gated[h] = per_piece.tile([P, CH_BLOCKS, PIECE], F32, name="gated")
             for part in range(PIECE_CHUNKS):
                 apply_gate(h, part)

@@ -86,6 +86,14 @@ def tile_sequenceframetransformerupdate_kernel(tc, s, cond_gain, wc1, bc1, wcn, 
         def bank(name):
             return psum.tile([P, PIECE], F32, name=name, tag="bank")
 
+        zeros = held.tile([P, PIECE], BF16, name="zeros")
+        nc.vector.memset(zeros[:], 0.0)
+        idle_ps = bank("idle_ps")
+
+        def keep_clock(count):
+            for k in range(count):
+                nc.tensor.matmul(idle_ps[:], zeros[:, 0:P], zeros[:], start=True, stop=True)
+
         def load_table_of(func, column, name):
             scratch = held.tile([P, 1], F32, name=name)
             nc.scalar.activation(scratch[:], column, func)
@@ -183,15 +191,19 @@ def tile_sequenceframetransformerupdate_kernel(tc, s, cond_gain, wc1, bc1, wcn, 
                 nc.sync.dma_start(out[m * P : (m + 1) * P, first : first + CHUNK], result[:])
 
         load_table_of(FUNC.Sqrt, eps_col[:], "scratch_sqrt")
+        keep_clock(5)
         for c in range(EARLY_CHUNKS):
             flip_forward(c)
+        keep_clock(2)
         for part in range(S_PARTS):
             residue_moments(part)
         load_table_of(FUNC.Sigmoid, s_std[:, S_BLOCKS - 1, :], "scratch_sigmoid")
         for part in range(S_PARTS):
             residue_window(part)
+        keep_clock(2)
         for c in range(EARLY_CHUNKS, N_CHUNKS):
             flip_forward(c)
+        keep_clock(2)
         for c in range(N_CHUNKS):
             frame_moments(c)
         for h in range(N_PIECES):

@@ -79,20 +79,12 @@ def tile_sequenceframetransformerupdate_kernel(tc, s, cond_gain, wc1, bc1, wcn, 
         s_norm = held.tile([P, S_BLOCKS, D], F32, name="s_norm")
         cn = held.tile([D, S], BF16, name="cn")
         gate = held.tile([P, CH_BLOCKS, N], F32, name="gate")
-        flipped, rstd, offset, snT, sn_ps = {}, {}, {}, {}, {}
+        flipped, rstd, recentre, snT, sn_ps = {}, {}, {}, {}, {}
         gate_ps, shift_ps = {}, {}
         gated = {}
 
         def bank(name):
             return psum.tile([P, PIECE], F32, name=name, tag="bank")
-
-        zeros = held.tile([P, PIECE], BF16, name="zeros")
-        nc.vector.memset(zeros[:], 0.0)
-        idle_ps = bank("idle_ps")
-
-        def keep_clock(count):
-            for k in range(count):
-                nc.tensor.matmul(idle_ps[:], zeros[:, 0:P], zeros[:], start=True, stop=True)
 
         def load_table_of(func, column, name):
             scratch = held.tile([P, 1], F32, name=name)
@@ -104,12 +96,12 @@ def tile_sequenceframetransformerupdate_kernel(tc, s, cond_gain, wc1, bc1, wcn, 
                 nc.vector.bn_stats(s_stats[:, b, :], s_rows[:, b, :])
             for b in blocks:
                 nc.vector.bn_aggr(s_mean_var[:, b, :], s_stats[:, b, :])
-            both = slice(part * PART_BLOCKS, (part + 1) * PART_BLOCKS)
-            nc.scalar.activation(s_std[:, both, :], s_mean_var[:, both, 1:2], FUNC.Sqrt, bias=eps_col[:, 0:1])
+            span = slice(part * PART_BLOCKS, (part + 1) * PART_BLOCKS)
+            nc.scalar.activation(s_std[:, span, :], s_mean_var[:, span, 1:2], FUNC.Sqrt, bias=eps_col[:, 0:1])
 
         def residue_window(part):
-            both = slice(part * PART_BLOCKS, (part + 1) * PART_BLOCKS)
-            nc.vector.reciprocal(s_rstd[:, both, :], s_std[:, both, :])
+            span = slice(part * PART_BLOCKS, (part + 1) * PART_BLOCKS)
+            nc.vector.reciprocal(s_rstd[:, span, :], s_std[:, span, :])
             sT_ps = bank("sT_ps")
             for k in range(PART_BLOCKS):
                 b = part * PART_BLOCKS + k
@@ -127,7 +119,7 @@ def tile_sequenceframetransformerupdate_kernel(tc, s, cond_gain, wc1, bc1, wcn, 
             )
 
         def flip_forward(c):
-            flipped[c] = bank("flipped").rearrange("p (q m) -> p q m", q=FR_BLOCKS)
+            flipped[c] = bank("flipped").rearrange("p (q ch) -> p q ch", q=FR_BLOCKS)
             for q in range(FR_BLOCKS):
                 for m in range(CH_BLOCKS):
                     nc.tensor.transpose(
@@ -144,14 +136,18 @@ def tile_sequenceframetransformerupdate_kernel(tc, s, cond_gain, wc1, bc1, wcn, 
             nc.gpsimd.tensor_tensor(rstd[c][:], mean_var[:, :, 1:2], neg_half[:], op=ALU.pow)
             neg_mean = per_chunk.tile([P, FR_BLOCKS, 1], F32, name="neg_mean")
             nc.vector.tensor_scalar(neg_mean[:], mean_var[:, :, 0:1], -1.0, None, op0=ALU.mult)
-            offset[c] = per_chunk.tile([P, FR_BLOCKS, 1], F32, name="offset")
-            nc.gpsimd.tensor_tensor(offset[c][:], neg_mean[:], rstd[c][:], op=ALU.mult)
+            recentre[c] = per_chunk.tile([P, FR_BLOCKS, 1], F32, name="recentre")
+            nc.gpsimd.tensor_tensor(recentre[c][:], neg_mean[:], rstd[c][:], op=ALU.mult)
 
         def normalise(c):
             snT[c] = per_chunk.tile([P, FR_BLOCKS, CS], F32, name="snT")
             for q in range(FR_BLOCKS):
                 nc.scalar.activation(
-                    snT[c][:, q, :], flipped[c][:, q, :], FUNC.Identity, bias=offset[c][:, q, :], scale=rstd[c][:, q, :]
+                    snT[c][:, q, :],
+                    flipped[c][:, q, :],
+                    FUNC.Identity,
+                    bias=recentre[c][:, q, :],
+                    scale=rstd[c][:, q, :],
                 )
 
         def flip_back(c):
@@ -173,37 +169,30 @@ def tile_sequenceframetransformerupdate_kernel(tc, s, cond_gain, wc1, bc1, wcn, 
                 gate[:, m, h * PIECE : (h + 1) * PIECE], gate_ps[h, m][:], FUNC.Sigmoid, bias=bias[:, m : m + 1]
             )
 
-        def apply_gate(h, part):
-            c = h * PIECE_CHUNKS + part
+        def apply_gate(c):
+            h, place = divmod(c, PIECE_CHUNKS)
             nc.vector.tensor_tensor(
-                gated[h][:, :, part * CHUNK : (part + 1) * CHUNK],
+                gated[h][:, :, place * CHUNK : (place + 1) * CHUNK],
                 sn_ps[c][:],
                 gate[:, :, c * CHUNK : (c + 1) * CHUNK],
                 op=ALU.mult,
             )
 
         def add_shift(h, m):
-            for part in range(PIECE_CHUNKS):
-                cols = slice(part * CHUNK, (part + 1) * CHUNK)
-                result = per_chunk.tile([P, CHUNK], F32, name="result")
-                nc.vector.tensor_tensor(result[:], gated[h][:, m, cols], shift_ps[h, m][:, cols], op=ALU.add)
-                first = h * PIECE + part * CHUNK
-                nc.sync.dma_start(out[m * P : (m + 1) * P, first : first + CHUNK], result[:])
+            result = per_chunk.tile([P, PIECE], F32, name="result")
+            nc.vector.tensor_tensor(result[:], gated[h][:, m, :], shift_ps[h, m][:], op=ALU.add)
+            nc.sync.dma_start(out[m * P : (m + 1) * P, h * PIECE : (h + 1) * PIECE], result[:])
 
         load_table_of(FUNC.Sqrt, eps_col[:], "scratch_sqrt")
-        keep_clock(5)
         for c in range(EARLY_CHUNKS):
             flip_forward(c)
-        keep_clock(2)
         for part in range(S_PARTS):
             residue_moments(part)
         load_table_of(FUNC.Sigmoid, s_std[:, S_BLOCKS - 1, :], "scratch_sigmoid")
         for part in range(S_PARTS):
             residue_window(part)
-        keep_clock(2)
         for c in range(EARLY_CHUNKS, N_CHUNKS):
             flip_forward(c)
-        keep_clock(2)
         for c in range(N_CHUNKS):
             frame_moments(c)
         for h in range(N_PIECES):
@@ -220,7 +209,7 @@ def tile_sequenceframetransformerupdate_kernel(tc, s, cond_gain, wc1, bc1, wcn, 
                 shift_ps[h, m] = project(wcn_sb, h, m, "shift_ps")
         for h in range(N_PIECES):
             gated[h] = per_piece.tile([P, CH_BLOCKS, PIECE], F32, name="gated")
-            for part in range(PIECE_CHUNKS):
-                apply_gate(h, part)
+            for c in range(h * PIECE_CHUNKS, (h + 1) * PIECE_CHUNKS):
+                apply_gate(c)
             for m in range(CH_BLOCKS):
                 add_shift(h, m)

@@ -42,7 +42,6 @@ def tile_sequenceframetransformerupdate_kernel(tc, s, cond_gain, wc1, bc1, wcn, 
     with (
         tc.tile_pool(name="held", bufs=1) as held,
         tc.tile_pool(name="per_chunk", bufs=N_CHUNKS) as per_chunk,
-        tc.tile_pool(name="per_piece", bufs=N_PIECES) as per_piece,
         tc.psum_pool(name="psum", bufs=BANKS) as psum,
     ):
         gain = held.tile([D, 1], F32, name="gain")
@@ -79,8 +78,8 @@ def tile_sequenceframetransformerupdate_kernel(tc, s, cond_gain, wc1, bc1, wcn, 
         s_norm = held.tile([P, S_BLOCKS, D], F32, name="s_norm")
         cn = held.tile([D, S], BF16, name="cn")
         gate = held.tile([P, CH_BLOCKS, N], F32, name="gate")
-        flipped, rstd, recentre, snT, sn_ps = {}, {}, {}, {}, {}
-        gate_ps, shift_ps = {}, {}
+        flipped, rstd, recentre, snT = {}, {}, {}, {}
+        gate_ps, shift_ps, sn_ps = {}, {}, {}
         gated = {}
 
         def bank(name):
@@ -150,12 +149,15 @@ def tile_sequenceframetransformerupdate_kernel(tc, s, cond_gain, wc1, bc1, wcn, 
                     scale=rstd[c][:, q, :],
                 )
 
-        def flip_back(c):
-            sn_ps[c] = bank("sn_ps").rearrange("p (m j) -> p m j", m=CH_BLOCKS)
-            for m in range(CH_BLOCKS):
+        def flip_back(h, m):
+            sn_ps[h, m] = bank("sn_ps")
+            for k in range(PIECE_CHUNKS):
                 for q in range(FR_BLOCKS):
+                    first = (k * FR_BLOCKS + q) * P
                     nc.tensor.transpose(
-                        sn_ps[c][:, m, q * P : (q + 1) * P], snT[c][:, q, m * P : (m + 1) * P], ident[:]
+                        sn_ps[h, m][:, first : first + P],
+                        snT[h * PIECE_CHUNKS + k][:, q, m * P : (m + 1) * P],
+                        ident[:],
                     )
 
         def project(weights, h, m, name):
@@ -169,18 +171,15 @@ def tile_sequenceframetransformerupdate_kernel(tc, s, cond_gain, wc1, bc1, wcn, 
                 gate[:, m, h * PIECE : (h + 1) * PIECE], gate_ps[h, m][:], FUNC.Sigmoid, bias=bias[:, m : m + 1]
             )
 
-        def apply_gate(c):
-            h, place = divmod(c, PIECE_CHUNKS)
+        def apply_gate(h, m):
+            gated[h, m] = per_chunk.tile([P, PIECE], F32, name="gated")
             nc.vector.tensor_tensor(
-                gated[h][:, :, place * CHUNK : (place + 1) * CHUNK],
-                sn_ps[c][:],
-                gate[:, :, c * CHUNK : (c + 1) * CHUNK],
-                op=ALU.mult,
+                gated[h, m][:], sn_ps[h, m][:], gate[:, m, h * PIECE : (h + 1) * PIECE], op=ALU.mult
             )
 
         def add_shift(h, m):
             result = per_chunk.tile([P, PIECE], F32, name="result")
-            nc.vector.tensor_tensor(result[:], gated[h][:, m, :], shift_ps[h, m][:], op=ALU.add)
+            nc.vector.tensor_tensor(result[:], gated[h, m][:], shift_ps[h, m][:], op=ALU.add)
             nc.sync.dma_start(out[m * P : (m + 1) * P, h * PIECE : (h + 1) * PIECE], result[:])
 
         load_table_of(FUNC.Sqrt, eps_col[:], "scratch_sqrt")
@@ -195,21 +194,13 @@ def tile_sequenceframetransformerupdate_kernel(tc, s, cond_gain, wc1, bc1, wcn, 
             flip_forward(c)
         for c in range(N_CHUNKS):
             frame_moments(c)
-        for h in range(N_PIECES):
-            chunks = range(h * PIECE_CHUNKS, (h + 1) * PIECE_CHUNKS)
-            for c in chunks:
-                normalise(c)
-            for m in range(CH_BLOCKS):
-                gate_ps[h, m] = project(wc1_sb, h, m, "gate_ps")
-            for c in chunks:
-                flip_back(c)
-            for m in range(CH_BLOCKS):
-                sigmoid(h, m)
-            for m in range(CH_BLOCKS):
-                shift_ps[h, m] = project(wcn_sb, h, m, "shift_ps")
-        for h in range(N_PIECES):
-            gated[h] = per_piece.tile([P, CH_BLOCKS, PIECE], F32, name="gated")
-            for c in range(h * PIECE_CHUNKS, (h + 1) * PIECE_CHUNKS):
-                apply_gate(c)
-            for m in range(CH_BLOCKS):
-                add_shift(h, m)
+            normalise(c)
+        blocks = [(h, m) for h in range(N_PIECES) for m in range(CH_BLOCKS)]
+        for h, m in blocks:
+            gate_ps[h, m] = project(wc1_sb, h, m, "gate_ps")
+            sigmoid(h, m)
+        for h, m in blocks:
+            flip_back(h, m)
+            shift_ps[h, m] = project(wcn_sb, h, m, "shift_ps")
+            apply_gate(h, m)
+            add_shift(h, m)

@@ -78,7 +78,7 @@ def tile_sequenceframetransformerupdate_kernel(tc, s, cond_gain, wc1, bc1, wcn, 
         s_norm = held.tile([P, S_BLOCKS, D], F32, name="s_norm")
         cn = held.tile([D, S], BF16, name="cn")
         gate = held.tile([P, CH_BLOCKS, N], F32, name="gate")
-        flipped, rstd, recentre, snT = {}, {}, {}, {}
+        flipped, rstd, neg_mean, recentre, snT = {}, {}, {}, {}, {}
         gate_ps, shift_ps, sn_ps = {}, {}, {}
         gated = {}
 
@@ -133,12 +133,13 @@ def tile_sequenceframetransformerupdate_kernel(tc, s, cond_gain, wc1, bc1, wcn, 
                 nc.vector.bn_aggr(mean_var[:, q, :], frame_stats[:, c * FR_BLOCKS + q, :])
             rstd[c] = per_chunk.tile([P, FR_BLOCKS, 1], F32, name="rstd")
             nc.gpsimd.tensor_tensor(rstd[c][:], mean_var[:, :, 1:2], neg_half[:], op=ALU.pow)
-            neg_mean = per_chunk.tile([P, FR_BLOCKS, 1], F32, name="neg_mean")
-            nc.vector.tensor_scalar(neg_mean[:], mean_var[:, :, 0:1], -1.0, None, op0=ALU.mult)
-            recentre[c] = per_chunk.tile([P, FR_BLOCKS, 1], F32, name="recentre")
-            nc.gpsimd.tensor_tensor(recentre[c][:], neg_mean[:], rstd[c][:], op=ALU.mult)
+            neg_mean[c] = per_chunk.tile([P, FR_BLOCKS, 1], F32, name="neg_mean")
+            nc.vector.tensor_scalar(neg_mean[c][:], mean_var[:, :, 0:1], -1.0, None, op0=ALU.mult)
 
         def normalise(c):
+            recentre[c] = per_chunk.tile([P, FR_BLOCKS, 1], F32, name="recentre")
+            for q in range(FR_BLOCKS):
+                nc.scalar.activation(recentre[c][:, q, :], neg_mean[c][:, q, :], FUNC.Identity, scale=rstd[c][:, q, :])
             snT[c] = per_chunk.tile([P, FR_BLOCKS, CS], F32, name="snT")
             for q in range(FR_BLOCKS):
                 nc.scalar.activation(

@@ -200,8 +200,12 @@ def tile_sequenceframetransformerupdate_kernel(tc, s, cond_gain, wc1, bc1, wcn, 
         for h, m in blocks:
             gate_ps[h, m] = project(wc1_sb, h, m, "gate_ps")
             sigmoid(h, m)
-        for h, m in blocks:
-            flip_back(h, m)
-            shift_ps[h, m] = project(wcn_sb, h, m, "shift_ps")
-            apply_gate(h, m)
-            add_shift(h, m)
+        for h in range(N_PIECES):
+            for m in range(CH_BLOCKS):
+                flip_back(h, m)
+            for m in range(CH_BLOCKS):
+                shift_ps[h, m] = project(wcn_sb, h, m, "shift_ps")
+            for m in range(CH_BLOCKS):
+                apply_gate(h, m)
+            for m in range(CH_BLOCKS):
+                add_shift(h, m)

@@ -183,6 +183,15 @@ def tile_sequenceframetransformerupdate_kernel(tc, s, cond_gain, wc1, bc1, wcn, 
             nc.vector.tensor_tensor(result[:], gated[h, m][:], shift_ps[h, m][:], op=ALU.add)
             nc.sync.dma_start(out[m * P : (m + 1) * P, h * PIECE : (h + 1) * PIECE], result[:])
 
+        def add_shift_in_halves(h, m):
+            half = PIECE // 2
+            for k, queue in enumerate((nc.sync, nc.scalar)):
+                result = per_chunk.tile([P, half], F32, name="result_half")
+                span = slice(k * half, (k + 1) * half)
+                nc.vector.tensor_tensor(result[:], gated[h, m][:, span], shift_ps[h, m][:, span], op=ALU.add)
+                first = h * PIECE + k * half
+                queue.dma_start(out[m * P : (m + 1) * P, first : first + half], result[:])
+
         load_table_of(FUNC.Sqrt, eps_col[:], "scratch_sqrt")
         for c in range(EARLY_CHUNKS):
             flip_forward(c)
@@ -208,4 +217,7 @@ def tile_sequenceframetransformerupdate_kernel(tc, s, cond_gain, wc1, bc1, wcn, 
             for m in range(CH_BLOCKS):
                 apply_gate(h, m)
             for m in range(CH_BLOCKS):
-                add_shift(h, m)
+                if (h, m) == blocks[-1]:
+                    add_shift_in_halves(h, m)
+                else:
+                    add_shift(h, m)

@@ -73,7 +73,6 @@ def tile_sequenceframetransformerupdate_kernel(tc, s, cond_gain, wc1, bc1, wcn, 
 
         s_stats = held.tile([P, S_BLOCKS, STATS], F32, name="s_stats")
         s_mean_var = held.tile([P, S_BLOCKS, AGGR], F32, name="s_mean_var")
-        s_std = held.tile([P, S_BLOCKS, 1], F32, name="s_std")
         s_rstd = held.tile([P, S_BLOCKS, 1], F32, name="s_rstd")
         s_norm = held.tile([P, S_BLOCKS, D], F32, name="s_norm")
         cn = held.tile([D, S], BF16, name="cn")
@@ -96,11 +95,11 @@ def tile_sequenceframetransformerupdate_kernel(tc, s, cond_gain, wc1, bc1, wcn, 
             for b in blocks:
                 nc.vector.bn_aggr(s_mean_var[:, b, :], s_stats[:, b, :])
             span = slice(part * PART_BLOCKS, (part + 1) * PART_BLOCKS)
-            nc.scalar.activation(s_std[:, span, :], s_mean_var[:, span, 1:2], FUNC.Sqrt, bias=eps_col[:, 0:1])
+            nc.scalar.activation(
+                s_rstd[:, span, :], s_mean_var[:, span, 1:2], FUNC.Abs_reciprocal_sqrt, bias=eps_col[:, 0:1]
+            )
 
         def residue_window(part):
-            span = slice(part * PART_BLOCKS, (part + 1) * PART_BLOCKS)
-            nc.vector.reciprocal(s_rstd[:, span, :], s_std[:, span, :])
             sT_ps = bank("sT_ps")
             for k in range(PART_BLOCKS):
                 b = part * PART_BLOCKS + k
@@ -192,12 +191,12 @@ def tile_sequenceframetransformerupdate_kernel(tc, s, cond_gain, wc1, bc1, wcn, 
                 first = h * PIECE + k * half
                 queue.dma_start(out[m * P : (m + 1) * P, first : first + half], result[:])
 
-        load_table_of(FUNC.Sqrt, eps_col[:], "scratch_sqrt")
+        load_table_of(FUNC.Abs_reciprocal_sqrt, eps_col[:], "scratch_rsqrt")
         for c in range(EARLY_CHUNKS):
             flip_forward(c)
         for part in range(S_PARTS):
             residue_moments(part)
-        load_table_of(FUNC.Sigmoid, s_std[:, S_BLOCKS - 1, :], "scratch_sigmoid")
+        load_table_of(FUNC.Sigmoid, s_rstd[:, S_BLOCKS - 1, :], "scratch_sigmoid")
         for part in range(S_PARTS):
             residue_window(part)
         for c in range(EARLY_CHUNKS, N_CHUNKS):

@@ -44,20 +44,21 @@ def tile_sequenceframetransformerupdate_kernel(tc, s, cond_gain, wc1, bc1, wcn, 
         tc.tile_pool(name="per_chunk", bufs=N_CHUNKS) as per_chunk,
         tc.psum_pool(name="psum", bufs=BANKS) as psum,
     ):
+        rig_sb = [held.tile([P, CH_BLOCKS, CHUNK], F32, name=f"rig_sb{c}") for c in range(N_CHUNKS)]
+        nc.scalar.dma_start(rig_sb[0][:], rig_view[:, :, 0:CHUNK])
         gain = held.tile([D, 1], F32, name="gain")
         nc.scalar.dma_start(gain[:], cond_gain)
-        bias = held.tile([P, CH_BLOCKS], F32, name="bias")
-        with nc.allow_non_contiguous_dma(reason="256 biases, one to a partition and channel block"):
-            nc.scalar.dma_start(bias[:], bc1.rearrange("(m p) o -> p (m o)", p=P))
         s_rows = held.tile([P, S_BLOCKS, D], BF16, name="s_rows")
         nc.sync.dma_start(s_rows[:], s.rearrange("(b p) d -> p b d", p=P))
-        rig_sb = [held.tile([P, CH_BLOCKS, CHUNK], F32, name=f"rig_sb{c}") for c in range(N_CHUNKS)]
-        for c in range(N_CHUNKS):
+        for c in range(1, N_CHUNKS):
             nc.sync.dma_start(rig_sb[c][:], rig_view[:, :, c * CHUNK : (c + 1) * CHUNK])
         offsets = held.tile([P, N // 16], U16, name="offsets")
         nc.sync.dma_start(offsets[:], offs)
         wc1_sb = held.tile([D, CS], BF16, name="wc1_sb")
         nc.sync.dma_start(wc1_sb[:], wc1)
+        bias = held.tile([P, CH_BLOCKS], F32, name="bias")
+        with nc.allow_non_contiguous_dma(reason="256 biases, one to a partition and channel block"):
+            nc.sync.dma_start(bias[:], bc1.rearrange("(m p) o -> p (m o)", p=P))
         wcn_sb = held.tile([D, CS], BF16, name="wcn_sb")
         nc.sync.dma_start(wcn_sb[:], wcn)
 

@@ -49,7 +49,10 @@ def tile_sequenceframetransformerupdate_kernel(tc, s, cond_gain, wc1, bc1, wcn, 
         gain = held.tile([D, 1], F32, name="gain")
         nc.scalar.dma_start(gain[:], cond_gain)
         s_rows = held.tile([P, S_BLOCKS, D], BF16, name="s_rows")
-        nc.sync.dma_start(s_rows[:], s.rearrange("(b p) d -> p b d", p=P))
+        nc.sync.dma_start(
+            s_rows[:].rearrange("p (t b) d -> p t b d", t=S_PARTS),
+            s.rearrange("(t p b) d -> p t b d", t=S_PARTS, b=PART_BLOCKS),
+        )
         for c in range(1, N_CHUNKS):
             nc.sync.dma_start(rig_sb[c][:], rig_view[:, :, c * CHUNK : (c + 1) * CHUNK])
         offsets = held.tile([P, N // 16], U16, name="offsets")
@@ -114,7 +117,10 @@ def tile_sequenceframetransformerupdate_kernel(tc, s, cond_gain, wc1, bc1, wcn, 
                 )
                 nc.tensor.transpose(sT_ps[:, k * P : (k + 1) * P], s_norm[:, b, :], ident[:])
             nc.scalar.activation(
-                cn[:, part * PART : (part + 1) * PART], sT_ps[:, 0:PART], FUNC.Identity, scale=gain[:, 0:1]
+                cn[:, part * PART : (part + 1) * PART].rearrange("d (p b) -> d p b", b=PART_BLOCKS),
+                sT_ps[:, 0:PART].rearrange("d (b p) -> d p b", b=PART_BLOCKS),
+                FUNC.Identity,
+                scale=gain[:, 0:1],
             )
 
         def flip_forward(c):

import concourse.mybir as mybir
from concourse.masks import make_identity

F32 = mybir.dt.float32
BF16 = mybir.dt.bfloat16
U16 = mybir.dt.uint16
ALU = mybir.AluOpType
FUNC = mybir.ActivationFunctionType

P = 128
S = 512
D = 128
CS = 256
N = 1024
EPS = 1e-5

S_BLOCKS = S // P
S_PARTS = 2
PART = S // S_PARTS
PART_BLOCKS = S_BLOCKS // S_PARTS
CH_BLOCKS = CS // P
CHUNK = 256
N_CHUNKS = N // CHUNK
EARLY_CHUNKS = 2
FR_BLOCKS = CHUNK // P
PIECE = 512
N_PIECES = N // PIECE
PIECE_COLS = PIECE // 16
PIECE_CHUNKS = PIECE // CHUNK
BANKS = 8
GROUP = 3
STATS = 2 * GROUP
AGGR = 2

FLOPS = 2 * 2 * D * CS * N


def tile_sequenceframetransformerupdate_kernel(tc, s, cond_gain, wc1, bc1, wcn, rig, offs, out):
    nc = tc.nc
    rig_view = rig.rearrange("(m p) j -> p m j", p=P)

    with (
        tc.tile_pool(name="held", bufs=1) as held,
        tc.tile_pool(name="per_chunk", bufs=N_CHUNKS) as per_chunk,
        tc.psum_pool(name="psum", bufs=BANKS) as psum,
    ):
        rig_sb = [held.tile([P, CH_BLOCKS, CHUNK], F32, name=f"rig_sb{c}") for c in range(N_CHUNKS)]
        nc.scalar.dma_start(rig_sb[0][:], rig_view[:, :, 0:CHUNK])
        gain = held.tile([D, 1], F32, name="gain")
        nc.scalar.dma_start(gain[:], cond_gain)
        s_rows = held.tile([P, S_BLOCKS, D], BF16, name="s_rows")
        nc.sync.dma_start(
            s_rows[:].rearrange("p (t b) d -> p t b d", t=S_PARTS),
            s.rearrange("(t p b) d -> p t b d", t=S_PARTS, b=PART_BLOCKS),
        )
        for c in range(1, N_CHUNKS):
            nc.sync.dma_start(rig_sb[c][:], rig_view[:, :, c * CHUNK : (c + 1) * CHUNK])
        offsets = held.tile([P, N // 16], U16, name="offsets")
        nc.sync.dma_start(offsets[:], offs)
        wc1_sb = held.tile([D, CS], BF16, name="wc1_sb")
        nc.sync.dma_start(wc1_sb[:], wc1)
        bias = held.tile([P, CH_BLOCKS], F32, name="bias")
        with nc.allow_non_contiguous_dma(reason="256 biases, one to a partition and channel block"):
            nc.sync.dma_start(bias[:], bc1.rearrange("(m p) o -> p (m o)", p=P))
        wcn_sb = held.tile([D, CS], BF16, name="wcn_sb")
        nc.sync.dma_start(wcn_sb[:], wcn)

        ident = held.tile([P, P], F32, name="ident")
        make_identity(nc, ident[:])
        neg_half = held.tile([P, FR_BLOCKS, 1], F32, name="neg_half")
        nc.vector.memset(neg_half[:], -0.5)
        eps_col = held.tile([P, 1], F32, name="eps_col")
        nc.vector.memset(eps_col[:], EPS)
        frame_stats = held.tile([P, N // P, STATS + GROUP], F32, name="frame_stats")
        nc.vector.memset(frame_stats[:, :, STATS : STATS + 2], 0.0)
        nc.vector.memset(frame_stats[:, :, STATS + 2 : STATS + GROUP], CS * EPS)

        s_stats = held.tile([P, S_BLOCKS, STATS], F32, name="s_stats")
        s_mean_var = held.tile([P, S_BLOCKS, AGGR], F32, name="s_mean_var")
        s_rstd = held.tile([P, S_BLOCKS, 1], F32, name="s_rstd")
        s_norm = held.tile([P, S_BLOCKS, D], F32, name="s_norm")
        cn = held.tile([D, S], BF16, name="cn")
        gate = held.tile([P, CH_BLOCKS, N], F32, name="gate")
        flipped, rstd, neg_mean, recentre, snT = {}, {}, {}, {}, {}
        gate_ps, shift_ps, sn_ps = {}, {}, {}
        gated = {}

        def bank(name):
            return psum.tile([P, PIECE], F32, name=name, tag="bank")

        def load_table_of(func, column, name):
            scratch = held.tile([P, 1], F32, name=name)
            nc.scalar.activation(scratch[:], column, func)

        def residue_moments(part):
            blocks = range(part * PART_BLOCKS, (part + 1) * PART_BLOCKS)
            for b in blocks:
                nc.vector.bn_stats(s_stats[:, b, :], s_rows[:, b, :])
            for b in blocks:
                nc.vector.bn_aggr(s_mean_var[:, b, :], s_stats[:, b, :])
            span = slice(part * PART_BLOCKS, (part + 1) * PART_BLOCKS)
            nc.scalar.activation(
                s_rstd[:, span, :], s_mean_var[:, span, 1:2], FUNC.Abs_reciprocal_sqrt, bias=eps_col[:, 0:1]
            )

        def residue_window(part):
            sT_ps = bank("sT_ps")
            for k in range(PART_BLOCKS):
                b = part * PART_BLOCKS + k
                nc.vector.tensor_scalar(
                    s_norm[:, b, :],
                    s_rows[:, b, :],
                    s_mean_var[:, b, 0:1],
                    s_rstd[:, b, :],
                    op0=ALU.subtract,
                    op1=ALU.mult,
                )
                nc.tensor.transpose(sT_ps[:, k * P : (k + 1) * P], s_norm[:, b, :], ident[:])
            nc.scalar.activation(
                cn[:, part * PART : (part + 1) * PART].rearrange("d (p b) -> d p b", b=PART_BLOCKS),
                sT_ps[:, 0:PART].rearrange("d (b p) -> d p b", b=PART_BLOCKS),
                FUNC.Identity,
                scale=gain[:, 0:1],
            )

        def flip_forward(c):
            flipped[c] = bank("flipped").rearrange("p (q ch) -> p q ch", q=FR_BLOCKS)
            for q in range(FR_BLOCKS):
                for m in range(CH_BLOCKS):
                    nc.tensor.transpose(
                        flipped[c][:, q, m * P : (m + 1) * P], rig_sb[c][:, m, q * P : (q + 1) * P], ident[:]
                    )

        def frame_moments(c):
            mean_var = per_chunk.tile([P, FR_BLOCKS, AGGR], F32, name="mean_var")
            for q in range(FR_BLOCKS):
                nc.vector.bn_stats(frame_stats[:, c * FR_BLOCKS + q, 0:STATS], flipped[c][:, q, :])
            for q in range(FR_BLOCKS):
                nc.vector.bn_aggr(mean_var[:, q, :], frame_stats[:, c * FR_BLOCKS + q, :])
            rstd[c] = per_chunk.tile([P, FR_BLOCKS, 1], F32, name="rstd")
            nc.gpsimd.tensor_tensor(rstd[c][:], mean_var[:, :, 1:2], neg_half[:], op=ALU.pow)
            neg_mean[c] = per_chunk.tile([P, FR_BLOCKS, 1], F32, name="neg_mean")
            nc.vector.tensor_scalar(neg_mean[c][:], mean_var[:, :, 0:1], -1.0, None, op0=ALU.mult)

        def normalise(c):
            recentre[c] = per_chunk.tile([P, FR_BLOCKS, 1], F32, name="recentre")
            for q in range(FR_BLOCKS):
                nc.scalar.activation(recentre[c][:, q, :], neg_mean[c][:, q, :], FUNC.Identity, scale=rstd[c][:, q, :])
            snT[c] = per_chunk.tile([P, FR_BLOCKS, CS], F32, name="snT")
            for q in range(FR_BLOCKS):
                nc.scalar.activation(
                    snT[c][:, q, :],
                    flipped[c][:, q, :],
                    FUNC.Identity,
                    bias=recentre[c][:, q, :],
                    scale=rstd[c][:, q, :],
                )

        def flip_back(h, m):
            sn_ps[h, m] = bank("sn_ps")
            for k in range(PIECE_CHUNKS):
                for q in range(FR_BLOCKS):
                    first = (k * FR_BLOCKS + q) * P
                    nc.tensor.transpose(
                        sn_ps[h, m][:, first : first + P],
                        snT[h * PIECE_CHUNKS + k][:, q, m * P : (m + 1) * P],
                        ident[:],
                    )

        def project(weights, h, m, name):
            product = bank(name)
            piece = offsets[:, h * PIECE_COLS : (h + 1) * PIECE_COLS]
            nc.tensor.matmul(product[:], weights[:, m * P : (m + 1) * P], cn[:].indirect(piece), start=True, stop=True)
            return product

        def sigmoid(h, m):
            nc.scalar.activation(
                gate[:, m, h * PIECE : (h + 1) * PIECE], gate_ps[h, m][:], FUNC.Sigmoid, bias=bias[:, m : m + 1]
            )

        def apply_gate(h, m):
            gated[h, m] = per_chunk.tile([P, PIECE], F32, name="gated")
            nc.vector.tensor_tensor(
                gated[h, m][:], sn_ps[h, m][:], gate[:, m, h * PIECE : (h + 1) * PIECE], op=ALU.mult
            )

        def add_shift(h, m):
            result = per_chunk.tile([P, PIECE], F32, name="result")
            nc.vector.tensor_tensor(result[:], gated[h, m][:], shift_ps[h, m][:], op=ALU.add)
            nc.sync.dma_start(out[m * P : (m + 1) * P, h * PIECE : (h + 1) * PIECE], result[:])

        def add_shift_in_halves(h, m):
            half = PIECE // 2
            for k, queue in enumerate((nc.sync, nc.scalar)):
                result = per_chunk.tile([P, half], F32, name="result_half")
                span = slice(k * half, (k + 1) * half)
                nc.vector.tensor_tensor(result[:], gated[h, m][:, span], shift_ps[h, m][:, span], op=ALU.add)
                first = h * PIECE + k * half
                queue.dma_start(out[m * P : (m + 1) * P, first : first + half], result[:])

        load_table_of(FUNC.Abs_reciprocal_sqrt, eps_col[:], "scratch_rsqrt")
        for c in range(EARLY_CHUNKS):
            flip_forward(c)
        for part in range(S_PARTS):
            residue_moments(part)
        load_table_of(FUNC.Sigmoid, s_rstd[:, S_BLOCKS - 1, :], "scratch_sigmoid")
        for part in range(S_PARTS):
            residue_window(part)
        for c in range(EARLY_CHUNKS, N_CHUNKS):
            flip_forward(c)
        for c in range(N_CHUNKS):
            frame_moments(c)
            normalise(c)
        blocks = [(h, m) for h in range(N_PIECES) for m in range(CH_BLOCKS)]
        for h, m in blocks:
            gate_ps[h, m] = project(wc1_sb, h, m, "gate_ps")
            sigmoid(h, m)
        for h in range(N_PIECES):
            for m in range(CH_BLOCKS):
                flip_back(h, m)
            for m in range(CH_BLOCKS):
                shift_ps[h, m] = project(wcn_sb, h, m, "shift_ps")
            for m in range(CH_BLOCKS):
                apply_gate(h, m)
            for m in range(CH_BLOCKS):
                if (h, m) == blocks[-1]:
                    add_shift_in_halves(h, m)
                else:
                    add_shift(h, m)
